import numpy as np
import ml_dtypes


def mxq(x, axis, fmt="e4m3"):
    dtype, down = {"e4m3": (ml_dtypes.float8_e4m3fn, 7), "e5m2": (ml_dtypes.float8_e5m2, 14)}[fmt]
    v = np.moveaxis(np.asarray(x, np.float32).astype(ml_dtypes.bfloat16).astype(np.float64), axis, -1)
    blocks = v.reshape(v.shape[:-1] + (-1, 32))
    amax = np.abs(blocks).max(-1, keepdims=True)
    byte = np.maximum(np.where(amax > 0, np.frexp(amax)[1] - 1 + 127, 0) - down, 1)
    scale = np.exp2(byte - 127.0)
    codes = (blocks / scale).astype(np.float32).astype(dtype).astype(np.float64)
    return np.moveaxis((codes * scale).reshape(v.shape), -1, axis)


WIDE = False


def mx_kscale(k):
    if not WIDE:
        return np.ones(k)
    levels = np.array([10, -10, 5, -5, 0])
    a = np.random.permutation(np.resize(levels, k // 512 * 4)).reshape(k // 512, 4)
    idx = np.arange(k)
    return np.exp2(a[idx // 512, idx % 128 // 32])


BF16 = ml_dtypes.bfloat16


def bf(x):
    return np.asarray(x, np.float32).astype(BF16)


def f64(x):
    return np.asarray(x).astype(np.float64)


B, CIN, HID, FREQ, T, H = 1, 512, 256, 4, 128, 8
HD = HID * FREQ // H
EPS = 1e-5


def setup_inputs():
    s = mx_kscale(CIN)
    return {"x": bf(np.random.standard_normal((B, CIN, FREQ, T)) * s[None, :, None, None]),
            "qkv_w": bf(np.random.standard_normal((3 * HID, CIN)) / np.sqrt(CIN) / s[None, :]),
            "qkv_b": bf(np.random.standard_normal(3 * HID) * 0.2),
            "qkv_alpha": bf(0.25 + 0.05 * np.random.standard_normal(1)),
            "qkv_gamma": bf(1.0 + 0.1 * np.random.standard_normal((1, 3 * HID, 1, FREQ))),
            "qkv_beta": bf(0.1 * np.random.standard_normal((1, 3 * HID, 1, FREQ)))}


def reference(x, qkv_w, qkv_b, qkv_alpha, qkv_gamma, qkv_beta):
    xt = np.swapaxes(f64(x), -2, -1)
    y = (mxq(f64(qkv_w), 1, "e4m3") @ mxq(xt, 1, "e4m3").reshape(B, CIN, T * FREQ)).reshape(B, 3 * HID, T, FREQ)
    y = y + f64(qkv_b)[None, :, None, None]
    y = np.where(y >= 0, y, f64(qkv_alpha)[0] * y)
    mu = y.mean(axis=(1, 3), keepdims=True)
    var = np.square(y - mu).mean(axis=(1, 3), keepdims=True)
    n = (y - mu) / np.sqrt(var + EPS) * f64(qkv_gamma) + f64(qkv_beta)
    n = np.swapaxes(np.swapaxes(n, 1, 2).reshape(B, T, H, 3 * HD), 1, 2)
    return (np.ascontiguousarray(n[..., :HD]), np.ascontiguousarray(n[..., HD:2 * HD]), np.ascontiguousarray(n[..., 2 * HD:]))

@@ -1,0 +1,233 @@
+from contextlib import ExitStack
+
+import concourse.mybir as mybir
+from concourse.masks import make_identity
+
+F32 = mybir.dt.float32
+BF16 = mybir.dt.bfloat16
+U32 = mybir.dt.uint32
+U8 = mybir.dt.uint8
+FP8X4 = mybir.dt.float8_e4m3fn_x4
+ALU = mybir.AluOpType
+ACT = mybir.ActivationFunctionType
+AXIS = mybir.AxisListType
+
+P = 128
+PACK = 4
+CIN = P * PACK
+FREQ = 4
+CHANNELS = 768
+O_TILES = CHANNELS // P
+BANK = P * FREQ
+COLS = CHANNELS * FREQ
+HEAD_DIM = 128
+UNITS_PER_BANK = BANK // HEAD_DIM
+EPS = 1e-5
+
+FLOPS = 2 * CHANNELS * CIN * FREQ * P
+
+
+def tile_unified2dattentiononframe_pa_s_kernel(
+    tc, x, qkv_w, qkv_b, qkv_alpha, qkv_gamma, qkv_beta, out_0, out_1, out_2
+):
+    nc = tc.nc
+    out_views = [o.rearrange("a h t d -> t (a h) d") for o in (out_0, out_1, out_2)]
+
+    with ExitStack() as stack:
+        keep = stack.enter_context(tc.tile_pool(name="keep", bufs=1))
+        psum = stack.enter_context(tc.psum_pool(name="psum", bufs=8))
+
+        alpha_bc = keep.tile([P, 1], BF16)
+        nc.scalar.dma_start(out=alpha_bc[:], in_=qkv_alpha.partition_broadcast(P))
+        bias_bc = keep.tile([P, CHANNELS], BF16)
+        nc.scalar.dma_start(out=bias_bc[:], in_=qkv_b.partition_broadcast(P))
+
+        x_raw = keep.tile([P, PACK, BANK], BF16)
+        nc.sync.dma_start(
+            out=x_raw[:].rearrange("q (u e) w -> q u (e w)", u=2),
+            in_=x.rearrange("a (u q e) f t -> q (a u) (e f t)", u=2, e=2),
+        )
+        w_raw = keep.tile([P, O_TILES, CIN], BF16)
+        w_rows = qkv_w.rearrange("(j r) c -> r j c", r=P)
+        for pair in range(O_TILES // 2):
+            tiles = slice(2 * pair, 2 * pair + 2)
+            nc.sync.dma_start(out=w_raw[:, tiles, :], in_=w_rows[:, tiles, :])
+        gamma_bc = keep.tile([P, COLS], BF16)
+        nc.sync.dma_start(
+            out=gamma_bc[:],
+            in_=qkv_gamma.rearrange("a o b f -> (a o b f)").partition_broadcast(P),
+        )
+        beta_bc = keep.tile([P, COLS], BF16)
+        nc.sync.dma_start(
+            out=beta_bc[:],
+            in_=qkv_beta.rearrange("a o b f -> (a o b f)").partition_broadcast(P),
+        )
+
+        ident = keep.tile([P, P], F32)
+        make_identity(nc, ident[:])
+        one = keep.tile([P, 1], F32)
+        nc.vector.memset(one[:], 1.0)
+        warm = keep.tile([P, 1], F32)
+        nc.scalar.activation(out=warm[:], in_=one[:], func=ACT.Sqrt)
+
+        one_minus_alpha = keep.tile([P, 1], F32)
+        nc.vector.tensor_scalar(
+            out=one_minus_alpha[:], in0=alpha_bc[:], scalar1=-1.0, scalar2=1.0,
+            op0=ALU.mult, op1=ALU.add,
+        )
+
+        x_grouped = keep.tile([P, BANK, PACK], BF16, align_bytes=64)
+        for f in range(FREQ):
+            cols = slice(f * P, (f + 1) * P)
+            src = x_raw[:, :, cols].rearrange("q s w -> q w s")
+            if f < FREQ - 1:
+                nc.vector.tensor_copy(out=x_grouped[:, cols, :], in_=src)
+            else:
+                nc.scalar.copy(out=x_grouped[:, cols, :], in_=src)
+        x_codes = keep.tile([P, BANK], U32, align_bytes=64)
+        x_scales = keep.tile([P, BANK], U8, align_bytes=64)
+        nc.vector.quantize_mx(
+            out=x_codes[:].bitcast(FP8X4),
+            scales=x_scales[:],
+            in_=x_grouped[:].rearrange("q w s -> q (w s)"),
+        )
+
+        w_words = w_raw[:].rearrange("r j c -> r (j c)").bitcast(F32)
+        w_grouped = keep.tile([P, CHANNELS * PACK], BF16, align_bytes=64)
+        w_grouped_words = w_grouped[:].bitcast(F32).rearrange(
+            "q (j o u) -> q j o u", j=O_TILES, u=2
+        )
+        w_codes = keep.tile([P, CHANNELS], U32, align_bytes=64)
+        w_scales = keep.tile([P, CHANNELS], U8, align_bytes=64)
+
+        def prepare_w_pair(pair):
+            w_t = psum.tile([P, 2, 2, P], F32, tag="bank")
+            for i in range(2):
+                for u in range(2):
+                    first = (2 * pair + i) * (CIN // 2) + u * P
+                    nc.tensor.transpose(
+                        w_t[:, i, u, :], w_words[:, first : first + P], ident[:]
+                    )
+            nc.scalar.copy(
+                out=w_grouped_words[:, 2 * pair : 2 * pair + 2, :, :],
+                in_=w_t[:].rearrange("q i u o -> q i o u"),
+            )
+            cols = slice(2 * pair * P, (2 * pair + 2) * P)
+            nc.vector.quantize_mx(
+                out=w_codes[:, cols].bitcast(FP8X4),
+                scales=w_scales[:, cols],
+                in_=w_grouped[:, 2 * pair * P * PACK : (2 * pair + 2) * P * PACK],
+            )
+
+        y = keep.tile([P, COLS], F32)
+        neg_part = keep.tile([P, COLS], F32)
+        prelu = keep.tile([P, COLS], F32)
+        squares = keep.tile([P, COLS], F32)
+        sum_p = keep.tile([P, O_TILES], F32)
+        sum_sq = keep.tile([P, O_TILES], F32)
+        neg_shift = keep.tile([P, 1], F32)
+
+        def project(j):
+            cols = slice(j * BANK, (j + 1) * BANK)
+            z = psum.tile([P, FREQ, P], F32, tag="bank")
+            for f in range(FREQ):
+                nc.tensor.matmul_mx(
+                    out=z[:, f, :],
+                    lhsT=x_codes[:, f * P : (f + 1) * P].bitcast(FP8X4),
+                    lhsT_scale=x_scales[:, f * P : (f + 1) * P],
+                    rhs=w_codes[:, j * P : (j + 1) * P].bitcast(FP8X4),
+                    rhs_scale=w_scales[:, j * P : (j + 1) * P],
+                    start=True,
+                    stop=True,
+                )
+            nc.vector.tensor_tensor(
+                out=y[:, cols].rearrange("t (o f) -> t o f", f=FREQ),
+                in0=z[:].rearrange("t f o -> t o f"),
+                in1=bias_bc[:, j * P : (j + 1) * P].unsqueeze(2).to_broadcast([P, P, FREQ]),
+                op=ALU.add,
+            )
+            nc.scalar.activation(
+                out=neg_part[:, cols], in_=y[:, cols], func=ACT.Relu, scale=-1.0
+            )
+
+        def activate(j):
+            cols = slice(j * BANK, (j + 1) * BANK)
+            nc.vector.scalar_tensor_tensor(
+                out=prelu[:, cols], in0=neg_part[:, cols], scalar=one_minus_alpha[:, 0:1],
+                in1=y[:, cols], op0=ALU.mult, op1=ALU.add, accum_out=sum_p[:, j : j + 1],
+            )
+            if j == 0:
+                nc.vector.tensor_scalar(
+                    out=neg_shift[:], in0=sum_p[:, 0:1], scalar1=-1.0 / BANK, scalar2=None,
+                    op0=ALU.mult,
+                )
+            nc.scalar.activation(
+                out=squares[:, cols], in_=prelu[:, cols], func=ACT.Square,
+                bias=neg_shift[:, 0:1], scale=1.0, accum_out=sum_sq[:, j : j + 1],
+            )
+
+        for j in range(O_TILES + 1):
+            if j < O_TILES:
+                if j % 2 == 0:
+                    prepare_w_pair(j // 2)
+                project(j)
+            if j > 0:
+                activate(j - 1)
+
+        total_p = keep.tile([P, 1], F32)
+        nc.vector.tensor_reduce(out=total_p[:], in_=sum_p[:], axis=AXIS.X, op=ALU.add)
+        neg_mean = keep.tile([P, 1], F32)
+        nc.vector.tensor_scalar(
+            out=neg_mean[:], in0=total_p[:], scalar1=-1.0 / COLS, scalar2=None, op0=ALU.mult
+        )
+        offset = keep.tile([P, 1], F32)
+        nc.vector.tensor_tensor(
+            out=offset[:], in0=neg_shift[:], in1=neg_mean[:], op=ALU.subtract
+        )
+        offset_sq = keep.tile([P, 1], F32)
+        nc.vector.tensor_scalar(
+            out=offset_sq[:], in0=offset[:], scalar1=offset[:, 0:1], scalar2=EPS,
+            op0=ALU.mult, op1=ALU.subtract,
+        )
+
+        centred = keep.tile([P, COLS], F32)
+        result = keep.tile([P, COLS], F32)
+        rstd = keep.tile([P, 1], F32)
+
+        def gain(c):
+            cols = slice(c * BANK, (c + 1) * BANK)
+            nc.vector.scalar_tensor_tensor(
+                out=centred[:, cols], in0=prelu[:, cols], scalar=neg_mean[:, 0:1],
+                in1=gamma_bc[:, cols], op0=ALU.add, op1=ALU.mult,
+            )
+
+        def shift_and_store(c):
+            cols = slice(c * BANK, (c + 1) * BANK)
+            nc.vector.scalar_tensor_tensor(
+                out=result[:, cols], in0=centred[:, cols], scalar=rstd[:, 0:1],
+                in1=beta_bc[:, cols], op0=ALU.mult, op1=ALU.add,
+            )
+            for g in range(c * UNITS_PER_BANK, (c + 1) * UNITS_PER_BANK):
+                nc.sync.dma_start(
+                    out=out_views[g % 3][:, g // 3, :],
+                    in_=result[:, g * HEAD_DIM : (g + 1) * HEAD_DIM],
+                )
+
+        AHEAD = 2
+        for c in range(AHEAD):
+            gain(c)
+        total_sq = keep.tile([P, 1], F32)
+        nc.vector.tensor_reduce(out=total_sq[:], in_=sum_sq[:], axis=AXIS.X, op=ALU.add)
+        var_eps = keep.tile([P, 1], F32)
+        nc.vector.scalar_tensor_tensor(
+            out=var_eps[:], in0=total_sq[:], scalar=1.0 / COLS, in1=offset_sq[:],
+            op0=ALU.mult, op1=ALU.subtract,
+        )
+        std = keep.tile([P, 1], F32)
+        nc.scalar.activation(out=std[:], in_=var_eps[:], func=ACT.Sqrt)
+        for c in range(O_TILES):
+            if c + AHEAD < O_TILES:
+                gain(c + AHEAD)
+            if c == 0:
+                nc.vector.reciprocal(out=rstd[:], in_=std[:])
+            shift_and_store(c)

@@ -23,6 +23,13 @@ COLS = CHANNELS * FREQ
 HEAD_DIM = 128
 UNITS_PER_BANK = BANK // HEAD_DIM
 EPS = 1e-5
+ROW_VALUES = 2 * P
+BIAS_ROWS = CHANNELS // ROW_VALUES
+GAIN_ROWS = COLS // ROW_VALUES
+BIAS_ROW = 0
+GAMMA_ROW = BIAS_ROW + BIAS_ROWS
+BETA_ROW = GAMMA_ROW + GAIN_ROWS
+ROWS_PER_BANK = BANK // P
 
 FLOPS = 2 * CHANNELS * CIN * FREQ * P
 
@@ -39,8 +46,18 @@ def tile_unified2dattentiononframe_pa_s_kernel(
 
         alpha_bc = keep.tile([P, 1], BF16)
         nc.scalar.dma_start(out=alpha_bc[:], in_=qkv_alpha.partition_broadcast(P))
-        bias_bc = keep.tile([P, CHANNELS], BF16)
-        nc.scalar.dma_start(out=bias_bc[:], in_=qkv_b.partition_broadcast(P))
+        vec_rows = keep.tile([P, P], F32)
+        nc.vector.memset(vec_rows[:], 0.0)
+        vec_rows_bf = vec_rows[:].bitcast(BF16)
+        for first_row, n_rows, vec in (
+            (BIAS_ROW, BIAS_ROWS, qkv_b),
+            (GAMMA_ROW, GAIN_ROWS, qkv_gamma.rearrange("a o b f -> (a o b f)")),
+            (BETA_ROW, GAIN_ROWS, qkv_beta.rearrange("a o b f -> (a o b f)")),
+        ):
+            nc.scalar.dma_start(
+                out=vec_rows_bf[first_row : first_row + n_rows, :],
+                in_=vec.rearrange("(r w) -> r w", w=ROW_VALUES),
+            )
 
         x_raw = keep.tile([P, PACK, BANK], BF16)
         nc.sync.dma_start(
@@ -52,16 +69,6 @@ def tile_unified2dattentiononframe_pa_s_kernel(
         for pair in range(O_TILES // 2):
             tiles = slice(2 * pair, 2 * pair + 2)
             nc.sync.dma_start(out=w_raw[:, tiles, :], in_=w_rows[:, tiles, :])
-        gamma_bc = keep.tile([P, COLS], BF16)
-        nc.sync.dma_start(
-            out=gamma_bc[:],
-            in_=qkv_gamma.rearrange("a o b f -> (a o b f)").partition_broadcast(P),
-        )
-        beta_bc = keep.tile([P, COLS], BF16)
-        nc.sync.dma_start(
-            out=beta_bc[:],
-            in_=qkv_beta.rearrange("a o b f -> (a o b f)").partition_broadcast(P),
-        )
 
         ident = keep.tile([P, P], F32)
         make_identity(nc, ident[:])
@@ -75,6 +82,25 @@ def tile_unified2dattentiononframe_pa_s_kernel(
             out=one_minus_alpha[:], in0=alpha_bc[:], scalar1=-1.0, scalar2=1.0,
             op0=ALU.mult, op1=ALU.add,
         )
+
+        vec_cols_ps = psum.tile([P, P], F32, tag="bank")
+        nc.tensor.transpose(vec_cols_ps[:], vec_rows[:], ident[:])
+        vec_cols = keep.tile([P, BETA_ROW + GAIN_ROWS], F32)
+        nc.scalar.copy(out=vec_cols[:], in_=vec_cols_ps[:, 0 : BETA_ROW + GAIN_ROWS])
+
+        def spread_rows(bank, first_row, n_rows):
+            for r in range(n_rows):
+                nc.tensor.transpose(
+                    bank[:, r * P : (r + 1) * P],
+                    vec_cols[:, first_row + r : first_row + r + 1].to_broadcast([P, P]),
+                    ident[:],
+                )
+
+        bias_ps = psum.tile([P, BANK], F32, tag="bank")
+        spread_rows(bias_ps, BIAS_ROW, BIAS_ROWS)
+        bias_words = keep.tile([P, BIAS_ROWS * P], F32)
+        nc.scalar.copy(out=bias_words[:], in_=bias_ps[:, 0 : BIAS_ROWS * P])
+        bias_bc = bias_words[:].bitcast(BF16)
 
         x_grouped = keep.tile([P, BANK, PACK], BF16, align_bytes=64)
         for f in range(FREQ):
@@ -174,6 +200,14 @@ def tile_unified2dattentiononframe_pa_s_kernel(
             if j > 0:
                 activate(j - 1)
 
+        gamma_banks = []
+        beta_banks = []
+        for banks, first_row, label in ((gamma_banks, GAMMA_ROW, "gamma"), (beta_banks, BETA_ROW, "beta")):
+            for k in range(GAIN_ROWS // ROWS_PER_BANK):
+                bank = psum.tile([P, BANK], F32, tag="bank", name="%s%d" % (label, k))
+                spread_rows(bank, first_row + k * ROWS_PER_BANK, ROWS_PER_BANK)
+                banks.append(bank[:].bitcast(BF16))
+
         total_p = keep.tile([P, 1], F32)
         nc.vector.tensor_reduce(out=total_p[:], in_=sum_p[:], axis=AXIS.X, op=ALU.add)
         neg_mean = keep.tile([P, 1], F32)
@@ -198,14 +232,16 @@ def tile_unified2dattentiononframe_pa_s_kernel(
             cols = slice(c * BANK, (c + 1) * BANK)
             nc.vector.scalar_tensor_tensor(
                 out=centred[:, cols], in0=prelu[:, cols], scalar=neg_mean[:, 0:1],
-                in1=gamma_bc[:, cols], op0=ALU.add, op1=ALU.mult,
+                in1=gamma_banks[c // 2][:, (c % 2) * BANK : (c % 2 + 1) * BANK],
+                op0=ALU.add, op1=ALU.mult,
             )
 
         def shift_and_store(c):
             cols = slice(c * BANK, (c + 1) * BANK)
             nc.vector.scalar_tensor_tensor(
                 out=result[:, cols], in0=centred[:, cols], scalar=rstd[:, 0:1],
-                in1=beta_bc[:, cols], op0=ALU.mult, op1=ALU.add,
+                in1=beta_banks[c // 2][:, (c % 2) * BANK : (c % 2 + 1) * BANK],
+                op0=ALU.mult, op1=ALU.add,
             )
             for g in range(c * UNITS_PER_BANK, (c + 1) * UNITS_PER_BANK):
                 nc.sync.dma_start(

@@ -18,6 +18,7 @@ CIN = P * PACK
 FREQ = 4
 CHANNELS = 768
 O_TILES = CHANNELS // P
+PAIRS = O_TILES // 2
 BANK = P * FREQ
 COLS = CHANNELS * FREQ
 HEAD_DIM = 128
@@ -29,7 +30,11 @@ GAIN_ROWS = COLS // ROW_VALUES
 BIAS_ROW = 0
 GAMMA_ROW = BIAS_ROW + BIAS_ROWS
 BETA_ROW = GAMMA_ROW + GAIN_ROWS
+FILL_ROW = BETA_ROW + GAIN_ROWS
+FILL_ROWS = 32 - FILL_ROW
 ROWS_PER_BANK = BANK // P
+RUN = 4
+AHEAD = 3
 
 FLOPS = 2 * CHANNELS * CIN * FREQ * P
 
@@ -43,21 +48,7 @@ def tile_unified2dattentiononframe_pa_s_kernel(
     with ExitStack() as stack:
         keep = stack.enter_context(tc.tile_pool(name="keep", bufs=1))
         psum = stack.enter_context(tc.psum_pool(name="psum", bufs=8))
-
-        alpha_bc = keep.tile([P, 1], BF16)
-        nc.scalar.dma_start(out=alpha_bc[:], in_=qkv_alpha.partition_broadcast(P))
-        vec_rows = keep.tile([P, P], F32)
-        nc.vector.memset(vec_rows[:], 0.0)
-        vec_rows_bf = vec_rows[:].bitcast(BF16)
-        for first_row, n_rows, vec in (
-            (BIAS_ROW, BIAS_ROWS, qkv_b),
-            (GAMMA_ROW, GAIN_ROWS, qkv_gamma.rearrange("a o b f -> (a o b f)")),
-            (BETA_ROW, GAIN_ROWS, qkv_beta.rearrange("a o b f -> (a o b f)")),
-        ):
-            nc.scalar.dma_start(
-                out=vec_rows_bf[first_row : first_row + n_rows, :],
-                in_=vec.rearrange("(r w) -> r w", w=ROW_VALUES),
-            )
+        stack.enter_context(tc.manual_schedule())
 
         x_raw = keep.tile([P, PACK, BANK], BF16)
         nc.sync.dma_start(
@@ -66,9 +57,28 @@ def tile_unified2dattentiononframe_pa_s_kernel(
         )
         w_raw = keep.tile([P, O_TILES, CIN], BF16)
         w_rows = qkv_w.rearrange("(j r) c -> r j c", r=P)
-        for pair in range(O_TILES // 2):
+        for pair in range(PAIRS):
             tiles = slice(2 * pair, 2 * pair + 2)
             nc.sync.dma_start(out=w_raw[:, tiles, :], in_=w_rows[:, tiles, :])
+
+        vec_rows = keep.tile([P, P], F32)
+        vec_rows_bf = vec_rows[:].bitcast(BF16)
+        gamma_flat = qkv_gamma.rearrange("a o b f -> (a o b f)")
+        beta_flat = qkv_beta.rearrange("a o b f -> (a o b f)")
+        for first_row, n_rows, vec in (
+            (BIAS_ROW, BIAS_ROWS, qkv_b),
+            (GAMMA_ROW, GAIN_ROWS, gamma_flat),
+            (BETA_ROW, GAIN_ROWS, beta_flat),
+            (FILL_ROW, FILL_ROWS, gamma_flat),
+        ):
+            nc.scalar.dma_start(
+                out=vec_rows_bf[first_row : first_row + n_rows, :],
+                in_=vec.rearrange("(r w) -> r w", w=ROW_VALUES)[0:n_rows, :],
+            )
+        nc.gpsimd.memset(vec_rows[32:64, :], 0.0)
+        nc.gpsimd.memset(vec_rows[64:128, :], 0.0)
+        alpha_bc = keep.tile([P, 1], BF16)
+        nc.scalar.dma_start(out=alpha_bc[:], in_=qkv_alpha.partition_broadcast(P))
 
         ident = keep.tile([P, P], F32)
         make_identity(nc, ident[:])
@@ -77,39 +87,11 @@ def tile_unified2dattentiononframe_pa_s_kernel(
         warm = keep.tile([P, 1], F32)
         nc.scalar.activation(out=warm[:], in_=one[:], func=ACT.Sqrt)
 
-        one_minus_alpha = keep.tile([P, 1], F32)
-        nc.vector.tensor_scalar(
-            out=one_minus_alpha[:], in0=alpha_bc[:], scalar1=-1.0, scalar2=1.0,
-            op0=ALU.mult, op1=ALU.add,
-        )
-
-        vec_cols_ps = psum.tile([P, P], F32, tag="bank")
-        nc.tensor.transpose(vec_cols_ps[:], vec_rows[:], ident[:])
-        vec_cols = keep.tile([P, BETA_ROW + GAIN_ROWS], F32)
-        nc.scalar.copy(out=vec_cols[:], in_=vec_cols_ps[:, 0 : BETA_ROW + GAIN_ROWS])
-
-        def spread_rows(bank, first_row, n_rows):
-            for r in range(n_rows):
-                nc.tensor.transpose(
-                    bank[:, r * P : (r + 1) * P],
-                    vec_cols[:, first_row + r : first_row + r + 1].to_broadcast([P, P]),
-                    ident[:],
-                )
-
-        bias_ps = psum.tile([P, BANK], F32, tag="bank")
-        spread_rows(bias_ps, BIAS_ROW, BIAS_ROWS)
-        bias_words = keep.tile([P, BIAS_ROWS * P], F32)
-        nc.scalar.copy(out=bias_words[:], in_=bias_ps[:, 0 : BIAS_ROWS * P])
-        bias_bc = bias_words[:].bitcast(BF16)
-
         x_grouped = keep.tile([P, BANK, PACK], BF16, align_bytes=64)
-        for f in range(FREQ):
-            cols = slice(f * P, (f + 1) * P)
-            src = x_raw[:, :, cols].rearrange("q s w -> q w s")
-            if f < FREQ - 1:
-                nc.vector.tensor_copy(out=x_grouped[:, cols, :], in_=src)
-            else:
-                nc.scalar.copy(out=x_grouped[:, cols, :], in_=src)
+        nc.vector.tensor_copy(
+            out=x_grouped[:].rearrange("q (c i) s -> q c s i", i=RUN),
+            in_=x_raw[:].rearrange("q s (c i) -> q c s i", i=RUN),
+        )
         x_codes = keep.tile([P, BANK], U32, align_bytes=64)
         x_scales = keep.tile([P, BANK], U8, align_bytes=64)
         nc.vector.quantize_mx(
@@ -126,7 +108,7 @@ def tile_unified2dattentiononframe_pa_s_kernel(
         w_codes = keep.tile([P, CHANNELS], U32, align_bytes=64)
         w_scales = keep.tile([P, CHANNELS], U8, align_bytes=64)
 
-        def prepare_w_pair(pair):
+        def transpose_w_pair(pair):
             w_t = psum.tile([P, 2, 2, P], F32, tag="bank")
             for i in range(2):
                 for u in range(2):
@@ -138,6 +120,29 @@ def tile_unified2dattentiononframe_pa_s_kernel(
                 out=w_grouped_words[:, 2 * pair : 2 * pair + 2, :, :],
                 in_=w_t[:].rearrange("q i u o -> q i o u"),
             )
+
+        vec_cols = keep.tile([P, FILL_ROW], F32)
+
+        def spread_rows(bank, first_row, n_rows):
+            for r in range(n_rows):
+                nc.tensor.transpose(
+                    bank[:, r * P : (r + 1) * P],
+                    vec_cols[:, first_row + r : first_row + r + 1].to_broadcast([P, P]),
+                    ident[:],
+                )
+
+        transpose_w_pair(0)
+        vec_cols_ps = psum.tile([P, P], F32, tag="bank")
+        nc.tensor.transpose(vec_cols_ps[:], vec_rows[:], ident[:])
+        nc.scalar.copy(out=vec_cols[:], in_=vec_cols_ps[:, 0 : FILL_ROW])
+        transpose_w_pair(1)
+        bias_ps = psum.tile([P, BANK], F32, tag="bank")
+        spread_rows(bias_ps, BIAS_ROW, BIAS_ROWS)
+        bias_words = keep.tile([P, BIAS_ROWS * P], F32)
+        nc.scalar.copy(out=bias_words[:], in_=bias_ps[:, 0 : BIAS_ROWS * P])
+        bias_bc = bias_words[:].bitcast(BF16)
+
+        def quantise_w_pair(pair):
             cols = slice(2 * pair * P, (2 * pair + 2) * P)
             nc.vector.quantize_mx(
                 out=w_codes[:, cols].bitcast(FP8X4),
@@ -152,9 +157,12 @@ def tile_unified2dattentiononframe_pa_s_kernel(
         sum_p = keep.tile([P, O_TILES], F32)
         sum_sq = keep.tile([P, O_TILES], F32)
         neg_shift = keep.tile([P, 1], F32)
+        one_minus_alpha = keep.tile([P, 1], F32)
+        early_p = keep.tile([P, 1], F32)
 
-        def project(j):
-            cols = slice(j * BANK, (j + 1) * BANK)
+        products = {}
+
+        def multiply(j):
             z = psum.tile([P, FREQ, P], F32, tag="bank")
             for f in range(FREQ):
                 nc.tensor.matmul_mx(
@@ -166,9 +174,13 @@ def tile_unified2dattentiononframe_pa_s_kernel(
                     start=True,
                     stop=True,
                 )
+            products[j] = z
+
+        def add_bias(j):
+            cols = slice(j * BANK, (j + 1) * BANK)
             nc.vector.tensor_tensor(
                 out=y[:, cols].rearrange("t (o f) -> t o f", f=FREQ),
-                in0=z[:].rearrange("t f o -> t o f"),
+                in0=products[j][:].rearrange("t f o -> t o f"),
                 in1=bias_bc[:, j * P : (j + 1) * P].unsqueeze(2).to_broadcast([P, P, FREQ]),
                 op=ALU.add,
             )
@@ -183,49 +195,58 @@ def tile_unified2dattentiononframe_pa_s_kernel(
                 in1=y[:, cols], op0=ALU.mult, op1=ALU.add, accum_out=sum_p[:, j : j + 1],
             )
             if j == 0:
-                nc.vector.tensor_scalar(
-                    out=neg_shift[:], in0=sum_p[:, 0:1], scalar1=-1.0 / BANK, scalar2=None,
-                    op0=ALU.mult,
+                nc.gpsimd.tensor_scalar(
+                    out=neg_shift[:], in0=sum_p[:, 0:1], scalar1=-1.0 / BANK, scalar2=0.0,
+                    op0=ALU.mult, op1=ALU.add,
                 )
+
+        def square(j):
+            cols = slice(j * BANK, (j + 1) * BANK)
             nc.scalar.activation(
                 out=squares[:, cols], in_=prelu[:, cols], func=ACT.Square,
                 bias=neg_shift[:, 0:1], scale=1.0, accum_out=sum_sq[:, j : j + 1],
             )
 
-        for j in range(O_TILES + 1):
-            if j < O_TILES:
-                if j % 2 == 0:
-                    prepare_w_pair(j // 2)
-                project(j)
-            if j > 0:
-                activate(j - 1)
+        quantise_w_pair(0)
+        for s in range(O_TILES + 3):
+            if s < O_TILES:
+                multiply(s)
+            if s % 2 == 1 and (s + 3) // 2 < PAIRS:
+                transpose_w_pair((s + 3) // 2)
+            if s % 2 == 1 and (s + 1) // 2 < PAIRS:
+                quantise_w_pair((s + 1) // 2)
+            if s < O_TILES:
+                add_bias(s)
+            if s == 1:
+                nc.vector.tensor_scalar(
+                    out=one_minus_alpha[:], in0=alpha_bc[:], scalar1=-1.0, scalar2=1.0,
+                    op0=ALU.mult, op1=ALU.add,
+                )
+            if 2 <= s < O_TILES + 2:
+                activate(s - 2)
+            if s >= 3:
+                square(s - 3)
 
         gamma_banks = []
         beta_banks = []
-        for banks, first_row, label in ((gamma_banks, GAMMA_ROW, "gamma"), (beta_banks, BETA_ROW, "beta")):
+        for banks, first_row, label in (
+            (gamma_banks, GAMMA_ROW, "gamma"),
+            (beta_banks, BETA_ROW, "beta"),
+        ):
             for k in range(GAIN_ROWS // ROWS_PER_BANK):
                 bank = psum.tile([P, BANK], F32, tag="bank", name="%s%d" % (label, k))
                 spread_rows(bank, first_row + k * ROWS_PER_BANK, ROWS_PER_BANK)
                 banks.append(bank[:].bitcast(BF16))
 
-        total_p = keep.tile([P, 1], F32)
-        nc.vector.tensor_reduce(out=total_p[:], in_=sum_p[:], axis=AXIS.X, op=ALU.add)
-        neg_mean = keep.tile([P, 1], F32)
-        nc.vector.tensor_scalar(
-            out=neg_mean[:], in0=total_p[:], scalar1=-1.0 / COLS, scalar2=None, op0=ALU.mult
-        )
-        offset = keep.tile([P, 1], F32)
-        nc.vector.tensor_tensor(
-            out=offset[:], in0=neg_shift[:], in1=neg_mean[:], op=ALU.subtract
-        )
-        offset_sq = keep.tile([P, 1], F32)
-        nc.vector.tensor_scalar(
-            out=offset_sq[:], in0=offset[:], scalar1=offset[:, 0:1], scalar2=EPS,
-            op0=ALU.mult, op1=ALU.subtract,
-        )
-
         centred = keep.tile([P, COLS], F32)
         result = keep.tile([P, COLS], F32)
+        neg_mean = keep.tile([P, 1], F32)
+        offset = keep.tile([P, 1], F32)
+        neg_offset = keep.tile([P, 1], F32)
+        early_var = keep.tile([P, 1], F32)
+        early_sq = keep.tile([P, 1], F32)
+        rest = keep.tile([P, 1], F32)
+        std = keep.tile([P, 1], F32)
         rstd = keep.tile([P, 1], F32)
 
         def gain(c):
@@ -249,21 +270,38 @@ def tile_unified2dattentiononframe_pa_s_kernel(
                     in_=result[:, g * HEAD_DIM : (g + 1) * HEAD_DIM],
                 )
 
-        AHEAD = 2
-        for c in range(AHEAD):
-            gain(c)
-        total_sq = keep.tile([P, 1], F32)
-        nc.vector.tensor_reduce(out=total_sq[:], in_=sum_sq[:], axis=AXIS.X, op=ALU.add)
-        var_eps = keep.tile([P, 1], F32)
-        nc.vector.scalar_tensor_tensor(
-            out=var_eps[:], in0=total_sq[:], scalar=1.0 / COLS, in1=offset_sq[:],
-            op0=ALU.mult, op1=ALU.subtract,
+        last = O_TILES - 1
+        nc.vector.tensor_reduce(out=early_p[:], in_=sum_p[:, 0:last], axis=AXIS.X, op=ALU.add)
+        nc.vector.tensor_scalar(
+            out=neg_mean[:], in0=sum_p[:, last : last + 1], scalar1=early_p[:, 0:1],
+            scalar2=-1.0 / COLS, op0=ALU.add, op1=ALU.mult,
         )
-        std = keep.tile([P, 1], F32)
-        nc.scalar.activation(out=std[:], in_=var_eps[:], func=ACT.Sqrt)
+        gain(0)
+        nc.vector.tensor_reduce(
+            out=early_sq[:], in_=sum_sq[:, 0:last], axis=AXIS.X, op=ALU.add
+        )
+        nc.vector.tensor_tensor(
+            out=offset[:], in0=neg_shift[:], in1=neg_mean[:], op=ALU.subtract
+        )
+        nc.vector.tensor_tensor(
+            out=neg_offset[:], in0=neg_mean[:], in1=neg_shift[:], op=ALU.subtract
+        )
+        nc.vector.tensor_scalar(
+            out=early_var[:], in0=early_sq[:], scalar1=1.0 / COLS, scalar2=EPS,
+            op0=ALU.mult, op1=ALU.add,
+        )
+        gain(1)
+        nc.vector.scalar_tensor_tensor(
+            out=rest[:], in0=offset[:], scalar=neg_offset[:, 0:1], in1=early_var[:],
+            op0=ALU.mult, op1=ALU.add,
+        )
+        nc.scalar.activation(
+            out=std[:], in_=sum_sq[:, last : last + 1], func=ACT.Sqrt,
+            bias=rest[:, 0:1], scale=1.0 / COLS,
+        )
+        gain(2)
+        nc.vector.reciprocal(out=rstd[:], in_=std[:])
         for c in range(O_TILES):
             if c + AHEAD < O_TILES:
                 gain(c + AHEAD)
-            if c == 0:
-                nc.vector.reciprocal(out=rstd[:], in_=std[:])
             shift_and_store(c)

@@ -18,7 +18,6 @@ CIN = P * PACK
 FREQ = 4
 CHANNELS = 768
 O_TILES = CHANNELS // P
-PAIRS = O_TILES // 2
 BANK = P * FREQ
 COLS = CHANNELS * FREQ
 HEAD_DIM = 128
@@ -27,14 +26,12 @@ EPS = 1e-5
 ROW_VALUES = 2 * P
 BIAS_ROWS = CHANNELS // ROW_VALUES
 GAIN_ROWS = COLS // ROW_VALUES
-BIAS_ROW = 0
-GAMMA_ROW = BIAS_ROW + BIAS_ROWS
-BETA_ROW = GAMMA_ROW + GAIN_ROWS
-FILL_ROW = BETA_ROW + GAIN_ROWS
-FILL_ROWS = 32 - FILL_ROW
 ROWS_PER_BANK = BANK // P
 RUN = 4
 AHEAD = 3
+WARM_MATMULS = 4
+T_AHEAD = 4
+Q_AHEAD = 3
 
 FLOPS = 2 * CHANNELS * CIN * FREQ * P
 
@@ -50,6 +47,15 @@ def tile_unified2dattentiononframe_pa_s_kernel(
         psum = stack.enter_context(tc.psum_pool(name="psum", bufs=8))
         stack.enter_context(tc.manual_schedule())
 
+        def load_columns(queue, vec, n_rows, label):
+            columns = keep.tile([P, n_rows], F32, name=label)
+            queue.dma_start(
+                out=columns[:].bitcast(BF16).rearrange("w (r e) -> w r e", e=2),
+                in_=vec.rearrange("(r w e) -> w r e", w=P, e=2),
+            )
+            return columns
+
+        bias_cols = load_columns(nc.scalar, qkv_b, BIAS_ROWS, "bias_cols")
         x_raw = keep.tile([P, PACK, BANK], BF16)
         nc.sync.dma_start(
             out=x_raw[:].rearrange("q (u e) w -> q u (e w)", u=2),
@@ -57,28 +63,17 @@ def tile_unified2dattentiononframe_pa_s_kernel(
         )
         w_raw = keep.tile([P, O_TILES, CIN], BF16)
         w_rows = qkv_w.rearrange("(j r) c -> r j c", r=P)
-        for pair in range(PAIRS):
-            tiles = slice(2 * pair, 2 * pair + 2)
-            nc.sync.dma_start(out=w_raw[:, tiles, :], in_=w_rows[:, tiles, :])
+        for j in range(O_TILES):
+            nc.sync.dma_start(out=w_raw[:, j, :], in_=w_rows[:, j, :])
 
-        vec_rows = keep.tile([P, P], F32)
-        vec_rows_bf = vec_rows[:].bitcast(BF16)
-        gamma_flat = qkv_gamma.rearrange("a o b f -> (a o b f)")
-        beta_flat = qkv_beta.rearrange("a o b f -> (a o b f)")
-        for first_row, n_rows, vec in (
-            (BIAS_ROW, BIAS_ROWS, qkv_b),
-            (GAMMA_ROW, GAIN_ROWS, gamma_flat),
-            (BETA_ROW, GAIN_ROWS, beta_flat),
-            (FILL_ROW, FILL_ROWS, gamma_flat),
-        ):
-            nc.scalar.dma_start(
-                out=vec_rows_bf[first_row : first_row + n_rows, :],
-                in_=vec.rearrange("(r w) -> r w", w=ROW_VALUES)[0:n_rows, :],
-            )
-        nc.gpsimd.memset(vec_rows[32:64, :], 0.0)
-        nc.gpsimd.memset(vec_rows[64:128, :], 0.0)
         alpha_bc = keep.tile([P, 1], BF16)
         nc.scalar.dma_start(out=alpha_bc[:], in_=qkv_alpha.partition_broadcast(P))
+        gamma_cols = load_columns(
+            nc.sync, qkv_gamma.rearrange("a o b f -> (a o b f)"), GAIN_ROWS, "gamma_cols"
+        )
+        beta_cols = load_columns(
+            nc.sync, qkv_beta.rearrange("a o b f -> (a o b f)"), GAIN_ROWS, "beta_cols"
+        )
 
         ident = keep.tile([P, P], F32)
         make_identity(nc, ident[:])
@@ -87,11 +82,19 @@ def tile_unified2dattentiononframe_pa_s_kernel(
         warm = keep.tile([P, 1], F32)
         nc.scalar.activation(out=warm[:], in_=one[:], func=ACT.Sqrt)
 
+        warm_ps = psum.tile([P, P], F32, tag="bank")
+        for i in range(WARM_MATMULS):
+            nc.tensor.matmul(out=warm_ps[:], lhsT=ident[:], rhs=ident[:], start=True, stop=True)
+
         x_grouped = keep.tile([P, BANK, PACK], BF16, align_bytes=64)
-        nc.vector.tensor_copy(
-            out=x_grouped[:].rearrange("q (c i) s -> q c s i", i=RUN),
-            in_=x_raw[:].rearrange("q s (c i) -> q c s i", i=RUN),
-        )
+        for f in range(FREQ):
+            cols = slice(f * P, (f + 1) * P)
+            dst = x_grouped[:, cols, :].rearrange("q (c i) s -> q c s i", i=RUN)
+            src = x_raw[:, :, cols].rearrange("q s (c i) -> q c s i", i=RUN)
+            if f < FREQ - 1:
+                nc.vector.tensor_copy(out=dst, in_=src)
+            else:
+                nc.scalar.copy(out=dst, in_=src)
         x_codes = keep.tile([P, BANK], U32, align_bytes=64)
         x_scales = keep.tile([P, BANK], U8, align_bytes=64)
         nc.vector.quantize_mx(
@@ -108,46 +111,33 @@ def tile_unified2dattentiononframe_pa_s_kernel(
         w_codes = keep.tile([P, CHANNELS], U32, align_bytes=64)
         w_scales = keep.tile([P, CHANNELS], U8, align_bytes=64)
 
-        def transpose_w_pair(pair):
-            w_t = psum.tile([P, 2, 2, P], F32, tag="bank")
-            for i in range(2):
-                for u in range(2):
-                    first = (2 * pair + i) * (CIN // 2) + u * P
-                    nc.tensor.transpose(
-                        w_t[:, i, u, :], w_words[:, first : first + P], ident[:]
-                    )
+        def transpose_w(j):
+            w_t = psum.tile([P, 2, P], F32, tag="bank")
+            for u in range(2):
+                first = j * (CIN // 2) + u * P
+                nc.tensor.transpose(w_t[:, u, :], w_words[:, first : first + P], ident[:])
             nc.scalar.copy(
-                out=w_grouped_words[:, 2 * pair : 2 * pair + 2, :, :],
-                in_=w_t[:].rearrange("q i u o -> q i o u"),
+                out=w_grouped_words[:, j, :, :], in_=w_t[:].rearrange("q u o -> q o u")
             )
 
-        vec_cols = keep.tile([P, FILL_ROW], F32)
-
-        def spread_rows(bank, first_row, n_rows):
+        def spread_rows(bank, columns, first_row, n_rows):
             for r in range(n_rows):
                 nc.tensor.transpose(
                     bank[:, r * P : (r + 1) * P],
-                    vec_cols[:, first_row + r : first_row + r + 1].to_broadcast([P, P]),
+                    columns[:, first_row + r : first_row + r + 1].to_broadcast([P, P]),
                     ident[:],
                 )
 
-        transpose_w_pair(0)
-        vec_cols_ps = psum.tile([P, P], F32, tag="bank")
-        nc.tensor.transpose(vec_cols_ps[:], vec_rows[:], ident[:])
-        nc.scalar.copy(out=vec_cols[:], in_=vec_cols_ps[:, 0 : FILL_ROW])
-        transpose_w_pair(1)
         bias_ps = psum.tile([P, BANK], F32, tag="bank")
-        spread_rows(bias_ps, BIAS_ROW, BIAS_ROWS)
+        spread_rows(bias_ps, bias_cols, 0, BIAS_ROWS)
         bias_words = keep.tile([P, BIAS_ROWS * P], F32)
-        nc.scalar.copy(out=bias_words[:], in_=bias_ps[:, 0 : BIAS_ROWS * P])
         bias_bc = bias_words[:].bitcast(BF16)
 
-        def quantise_w_pair(pair):
-            cols = slice(2 * pair * P, (2 * pair + 2) * P)
+        def quantise_w(j):
             nc.vector.quantize_mx(
-                out=w_codes[:, cols].bitcast(FP8X4),
-                scales=w_scales[:, cols],
-                in_=w_grouped[:, 2 * pair * P * PACK : (2 * pair + 2) * P * PACK],
+                out=w_codes[:, j * P : (j + 1) * P].bitcast(FP8X4),
+                scales=w_scales[:, j * P : (j + 1) * P],
+                in_=w_grouped[:, j * BANK : (j + 1) * BANK],
             )
 
         y = keep.tile([P, COLS], F32)
@@ -207,16 +197,21 @@ def tile_unified2dattentiononframe_pa_s_kernel(
                 bias=neg_shift[:, 0:1], scale=1.0, accum_out=sum_sq[:, j : j + 1],
             )
 
-        quantise_w_pair(0)
+        for j in range(T_AHEAD):
+            transpose_w(j)
+            if j == Q_AHEAD - 1:
+                nc.scalar.copy(out=bias_words[:], in_=bias_ps[:, 0 : BIAS_ROWS * P])
+        for j in range(Q_AHEAD):
+            quantise_w(j)
         for s in range(O_TILES + 3):
             if s < O_TILES:
                 multiply(s)
-            if s % 2 == 1 and (s + 3) // 2 < PAIRS:
-                transpose_w_pair((s + 3) // 2)
-            if s % 2 == 1 and (s + 1) // 2 < PAIRS:
-                quantise_w_pair((s + 1) // 2)
+            if s + T_AHEAD < O_TILES:
+                transpose_w(s + T_AHEAD)
             if s < O_TILES:
                 add_bias(s)
+            if s + Q_AHEAD < O_TILES:
+                quantise_w(s + Q_AHEAD)
             if s == 1:
                 nc.vector.tensor_scalar(
                     out=one_minus_alpha[:], in0=alpha_bc[:], scalar1=-1.0, scalar2=1.0,
@@ -229,13 +224,13 @@ def tile_unified2dattentiononframe_pa_s_kernel(
 
         gamma_banks = []
         beta_banks = []
-        for banks, first_row, label in (
-            (gamma_banks, GAMMA_ROW, "gamma"),
-            (beta_banks, BETA_ROW, "beta"),
+        for banks, columns, label in (
+            (gamma_banks, gamma_cols, "gamma"),
+            (beta_banks, beta_cols, "beta"),
         ):
             for k in range(GAIN_ROWS // ROWS_PER_BANK):
                 bank = psum.tile([P, BANK], F32, tag="bank", name="%s%d" % (label, k))
-                spread_rows(bank, first_row + k * ROWS_PER_BANK, ROWS_PER_BANK)
+                spread_rows(bank, columns, k * ROWS_PER_BANK, ROWS_PER_BANK)
                 banks.append(bank[:].bitcast(BF16))
 
         centred = keep.tile([P, COLS], F32)

@@ -29,7 +29,6 @@ GAIN_ROWS = COLS // ROW_VALUES
 ROWS_PER_BANK = BANK // P
 RUN = 4
 AHEAD = 3
-WARM_MATMULS = 4
 T_AHEAD = 4
 Q_AHEAD = 3
 
@@ -81,10 +80,6 @@ def tile_unified2dattentiononframe_pa_s_kernel(
         nc.vector.memset(one[:], 1.0)
         warm = keep.tile([P, 1], F32)
         nc.scalar.activation(out=warm[:], in_=one[:], func=ACT.Sqrt)
-
-        warm_ps = psum.tile([P, P], F32, tag="bank")
-        for i in range(WARM_MATMULS):
-            nc.tensor.matmul(out=warm_ps[:], lhsT=ident[:], rhs=ident[:], start=True, stop=True)
 
         x_grouped = keep.tile([P, BANK, PACK], BF16, align_bytes=64)
         for f in range(FREQ):

@@ -292,6 +292,6 @@ def tile_unified2dattentiononframe_pa_s_kernel(
         gain(2)
         nc.vector.reciprocal(out=rstd[:], in_=std[:])
         for c in range(O_TILES):
-            if c + AHEAD < O_TILES:
-                gain(c + AHEAD)
+            if AHEAD <= c + 1 < O_TILES:
+                gain(c + 1)
             shift_and_store(c)

from contextlib import ExitStack

import concourse.mybir as mybir
from concourse.masks import make_identity

F32 = mybir.dt.float32
BF16 = mybir.dt.bfloat16
U32 = mybir.dt.uint32
U8 = mybir.dt.uint8
FP8X4 = mybir.dt.float8_e4m3fn_x4
ALU = mybir.AluOpType
ACT = mybir.ActivationFunctionType
AXIS = mybir.AxisListType

P = 128
PACK = 4
CIN = P * PACK
FREQ = 4
CHANNELS = 768
O_TILES = CHANNELS // P
BANK = P * FREQ
COLS = CHANNELS * FREQ
HEAD_DIM = 128
UNITS_PER_BANK = BANK // HEAD_DIM
EPS = 1e-5
ROW_VALUES = 2 * P
BIAS_ROWS = CHANNELS // ROW_VALUES
GAIN_ROWS = COLS // ROW_VALUES
ROWS_PER_BANK = BANK // P
RUN = 4
AHEAD = 3
T_AHEAD = 4
Q_AHEAD = 3

FLOPS = 2 * CHANNELS * CIN * FREQ * P


def tile_unified2dattentiononframe_pa_s_kernel(
    tc, x, qkv_w, qkv_b, qkv_alpha, qkv_gamma, qkv_beta, out_0, out_1, out_2
):
    nc = tc.nc
    out_views = [o.rearrange("a h t d -> t (a h) d") for o in (out_0, out_1, out_2)]

    with ExitStack() as stack:
        keep = stack.enter_context(tc.tile_pool(name="keep", bufs=1))
        psum = stack.enter_context(tc.psum_pool(name="psum", bufs=8))
        stack.enter_context(tc.manual_schedule())

        def load_columns(queue, vec, n_rows, label):
            columns = keep.tile([P, n_rows], F32, name=label)
            queue.dma_start(
                out=columns[:].bitcast(BF16).rearrange("w (r e) -> w r e", e=2),
                in_=vec.rearrange("(r w e) -> w r e", w=P, e=2),
            )
            return columns

        bias_cols = load_columns(nc.scalar, qkv_b, BIAS_ROWS, "bias_cols")
        x_raw = keep.tile([P, PACK, BANK], BF16)
        nc.sync.dma_start(
            out=x_raw[:].rearrange("q (u e) w -> q u (e w)", u=2),
            in_=x.rearrange("a (u q e) f t -> q (a u) (e f t)", u=2, e=2),
        )
        w_raw = keep.tile([P, O_TILES, CIN], BF16)
        w_rows = qkv_w.rearrange("(j r) c -> r j c", r=P)
        for j in range(O_TILES):
            nc.sync.dma_start(out=w_raw[:, j, :], in_=w_rows[:, j, :])

        alpha_bc = keep.tile([P, 1], BF16)
        nc.scalar.dma_start(out=alpha_bc[:], in_=qkv_alpha.partition_broadcast(P))
        gamma_cols = load_columns(
            nc.sync, qkv_gamma.rearrange("a o b f -> (a o b f)"), GAIN_ROWS, "gamma_cols"
        )
        beta_cols = load_columns(
            nc.sync, qkv_beta.rearrange("a o b f -> (a o b f)"), GAIN_ROWS, "beta_cols"
        )

        ident = keep.tile([P, P], F32)
        make_identity(nc, ident[:])
        one = keep.tile([P, 1], F32)
        nc.vector.memset(one[:], 1.0)
        warm = keep.tile([P, 1], F32)
        nc.scalar.activation(out=warm[:], in_=one[:], func=ACT.Sqrt)

        x_grouped = keep.tile([P, BANK, PACK], BF16, align_bytes=64)
        for f in range(FREQ):
            cols = slice(f * P, (f + 1) * P)
            dst = x_grouped[:, cols, :].rearrange("q (c i) s -> q c s i", i=RUN)
            src = x_raw[:, :, cols].rearrange("q s (c i) -> q c s i", i=RUN)
            if f < FREQ - 1:
                nc.vector.tensor_copy(out=dst, in_=src)
            else:
                nc.scalar.copy(out=dst, in_=src)
        x_codes = keep.tile([P, BANK], U32, align_bytes=64)
        x_scales = keep.tile([P, BANK], U8, align_bytes=64)
        nc.vector.quantize_mx(
            out=x_codes[:].bitcast(FP8X4),
            scales=x_scales[:],
            in_=x_grouped[:].rearrange("q w s -> q (w s)"),
        )

        w_words = w_raw[:].rearrange("r j c -> r (j c)").bitcast(F32)
        w_grouped = keep.tile([P, CHANNELS * PACK], BF16, align_bytes=64)
        w_grouped_words = w_grouped[:].bitcast(F32).rearrange(
            "q (j o u) -> q j o u", j=O_TILES, u=2
        )
        w_codes = keep.tile([P, CHANNELS], U32, align_bytes=64)
        w_scales = keep.tile([P, CHANNELS], U8, align_bytes=64)

        def transpose_w(j):
            w_t = psum.tile([P, 2, P], F32, tag="bank")
            for u in range(2):
                first = j * (CIN // 2) + u * P
                nc.tensor.transpose(w_t[:, u, :], w_words[:, first : first + P], ident[:])
            nc.scalar.copy(
                out=w_grouped_words[:, j, :, :], in_=w_t[:].rearrange("q u o -> q o u")
            )

        def spread_rows(bank, columns, first_row, n_rows):
            for r in range(n_rows):
                nc.tensor.transpose(
                    bank[:, r * P : (r + 1) * P],
                    columns[:, first_row + r : first_row + r + 1].to_broadcast([P, P]),
                    ident[:],
                )

        bias_ps = psum.tile([P, BANK], F32, tag="bank")
        spread_rows(bias_ps, bias_cols, 0, BIAS_ROWS)
        bias_words = keep.tile([P, BIAS_ROWS * P], F32)
        bias_bc = bias_words[:].bitcast(BF16)

        def quantise_w(j):
            nc.vector.quantize_mx(
                out=w_codes[:, j * P : (j + 1) * P].bitcast(FP8X4),
                scales=w_scales[:, j * P : (j + 1) * P],
                in_=w_grouped[:, j * BANK : (j + 1) * BANK],
            )

        y = keep.tile([P, COLS], F32)
        neg_part = keep.tile([P, COLS], F32)
        prelu = keep.tile([P, COLS], F32)
        squares = keep.tile([P, COLS], F32)
        sum_p = keep.tile([P, O_TILES], F32)
        sum_sq = keep.tile([P, O_TILES], F32)
        neg_shift = keep.tile([P, 1], F32)
        one_minus_alpha = keep.tile([P, 1], F32)
        early_p = keep.tile([P, 1], F32)

        products = {}

        def multiply(j):
            z = psum.tile([P, FREQ, P], F32, tag="bank")
            for f in range(FREQ):
                nc.tensor.matmul_mx(
                    out=z[:, f, :],
                    lhsT=x_codes[:, f * P : (f + 1) * P].bitcast(FP8X4),
                    lhsT_scale=x_scales[:, f * P : (f + 1) * P],
                    rhs=w_codes[:, j * P : (j + 1) * P].bitcast(FP8X4),
                    rhs_scale=w_scales[:, j * P : (j + 1) * P],
                    start=True,
                    stop=True,
                )
            products[j] = z

        def add_bias(j):
            cols = slice(j * BANK, (j + 1) * BANK)
            nc.vector.tensor_tensor(
                out=y[:, cols].rearrange("t (o f) -> t o f", f=FREQ),
                in0=products[j][:].rearrange("t f o -> t o f"),
                in1=bias_bc[:, j * P : (j + 1) * P].unsqueeze(2).to_broadcast([P, P, FREQ]),
                op=ALU.add,
            )
            nc.scalar.activation(
                out=neg_part[:, cols], in_=y[:, cols], func=ACT.Relu, scale=-1.0
            )

        def activate(j):
            cols = slice(j * BANK, (j + 1) * BANK)
            nc.vector.scalar_tensor_tensor(
                out=prelu[:, cols], in0=neg_part[:, cols], scalar=one_minus_alpha[:, 0:1],
                in1=y[:, cols], op0=ALU.mult, op1=ALU.add, accum_out=sum_p[:, j : j + 1],
            )
            if j == 0:
                nc.gpsimd.tensor_scalar(
                    out=neg_shift[:], in0=sum_p[:, 0:1], scalar1=-1.0 / BANK, scalar2=0.0,
                    op0=ALU.mult, op1=ALU.add,
                )

        def square(j):
            cols = slice(j * BANK, (j + 1) * BANK)
            nc.scalar.activation(
                out=squares[:, cols], in_=prelu[:, cols], func=ACT.Square,
                bias=neg_shift[:, 0:1], scale=1.0, accum_out=sum_sq[:, j : j + 1],
            )

        for j in range(T_AHEAD):
            transpose_w(j)
            if j == Q_AHEAD - 1:
                nc.scalar.copy(out=bias_words[:], in_=bias_ps[:, 0 : BIAS_ROWS * P])
        for j in range(Q_AHEAD):
            quantise_w(j)
        for s in range(O_TILES + 3):
            if s < O_TILES:
                multiply(s)
            if s + T_AHEAD < O_TILES:
                transpose_w(s + T_AHEAD)
            if s < O_TILES:
                add_bias(s)
            if s + Q_AHEAD < O_TILES:
                quantise_w(s + Q_AHEAD)
            if s == 1:
                nc.vector.tensor_scalar(
                    out=one_minus_alpha[:], in0=alpha_bc[:], scalar1=-1.0, scalar2=1.0,
                    op0=ALU.mult, op1=ALU.add,
                )
            if 2 <= s < O_TILES + 2:
                activate(s - 2)
            if s >= 3:
                square(s - 3)

        gamma_banks = []
        beta_banks = []
        for banks, columns, label in (
            (gamma_banks, gamma_cols, "gamma"),
            (beta_banks, beta_cols, "beta"),
        ):
            for k in range(GAIN_ROWS // ROWS_PER_BANK):
                bank = psum.tile([P, BANK], F32, tag="bank", name="%s%d" % (label, k))
                spread_rows(bank, columns, k * ROWS_PER_BANK, ROWS_PER_BANK)
                banks.append(bank[:].bitcast(BF16))

        centred = keep.tile([P, COLS], F32)
        result = keep.tile([P, COLS], F32)
        neg_mean = keep.tile([P, 1], F32)
        offset = keep.tile([P, 1], F32)
        neg_offset = keep.tile([P, 1], F32)
        early_var = keep.tile([P, 1], F32)
        early_sq = keep.tile([P, 1], F32)
        rest = keep.tile([P, 1], F32)
        std = keep.tile([P, 1], F32)
        rstd = keep.tile([P, 1], F32)

        def gain(c):
            cols = slice(c * BANK, (c + 1) * BANK)
            nc.vector.scalar_tensor_tensor(
                out=centred[:, cols], in0=prelu[:, cols], scalar=neg_mean[:, 0:1],
                in1=gamma_banks[c // 2][:, (c % 2) * BANK : (c % 2 + 1) * BANK],
                op0=ALU.add, op1=ALU.mult,
            )

        def shift_and_store(c):
            cols = slice(c * BANK, (c + 1) * BANK)
            nc.vector.scalar_tensor_tensor(
                out=result[:, cols], in0=centred[:, cols], scalar=rstd[:, 0:1],
                in1=beta_banks[c // 2][:, (c % 2) * BANK : (c % 2 + 1) * BANK],
                op0=ALU.mult, op1=ALU.add,
            )
            for g in range(c * UNITS_PER_BANK, (c + 1) * UNITS_PER_BANK):
                nc.sync.dma_start(
                    out=out_views[g % 3][:, g // 3, :],
                    in_=result[:, g * HEAD_DIM : (g + 1) * HEAD_DIM],
                )

        last = O_TILES - 1
        nc.vector.tensor_reduce(out=early_p[:], in_=sum_p[:, 0:last], axis=AXIS.X, op=ALU.add)
        nc.vector.tensor_scalar(
            out=neg_mean[:], in0=sum_p[:, last : last + 1], scalar1=early_p[:, 0:1],
            scalar2=-1.0 / COLS, op0=ALU.add, op1=ALU.mult,
        )
        gain(0)
        nc.vector.tensor_reduce(
            out=early_sq[:], in_=sum_sq[:, 0:last], axis=AXIS.X, op=ALU.add
        )
        nc.vector.tensor_tensor(
            out=offset[:], in0=neg_shift[:], in1=neg_mean[:], op=ALU.subtract
        )
        nc.vector.tensor_tensor(
            out=neg_offset[:], in0=neg_mean[:], in1=neg_shift[:], op=ALU.subtract
        )
        nc.vector.tensor_scalar(
            out=early_var[:], in0=early_sq[:], scalar1=1.0 / COLS, scalar2=EPS,
            op0=ALU.mult, op1=ALU.add,
        )
        gain(1)
        nc.vector.scalar_tensor_tensor(
            out=rest[:], in0=offset[:], scalar=neg_offset[:, 0:1], in1=early_var[:],
            op0=ALU.mult, op1=ALU.add,
        )
        nc.scalar.activation(
            out=std[:], in_=sum_sq[:, last : last + 1], func=ACT.Sqrt,
            bias=rest[:, 0:1], scale=1.0 / COLS,
        )
        gain(2)
        nc.vector.reciprocal(out=rstd[:], in_=std[:])
        for c in range(O_TILES):
            if AHEAD <= c + 1 < O_TILES:
                gain(c + 1)
            shift_and_store(c)
